import numpy as np
import ml_dtypes


def mxq(x, axis, fmt="e4m3"):
    dtype, down = {"e4m3": (ml_dtypes.float8_e4m3fn, 7), "e5m2": (ml_dtypes.float8_e5m2, 14)}[fmt]
    v = np.moveaxis(np.asarray(x, np.float32).astype(ml_dtypes.bfloat16).astype(np.float64), axis, -1)
    blocks = v.reshape(v.shape[:-1] + (-1, 32))
    amax = np.abs(blocks).max(-1, keepdims=True)
    byte = np.maximum(np.where(amax > 0, np.frexp(amax)[1] - 1 + 127, 0) - down, 1)
    scale = np.exp2(byte - 127.0)
    codes = (blocks / scale).astype(np.float32).astype(dtype).astype(np.float64)
    return np.moveaxis((codes * scale).reshape(v.shape), -1, axis)


WIDE = False


def mx_kscale(k):
    if not WIDE:
        return np.ones(k)
    levels = np.array([10, -10, 5, -5, 0])
    a = np.random.permutation(np.resize(levels, k // 512 * 4)).reshape(k // 512, 4)
    idx = np.arange(k)
    return np.exp2(a[idx // 512, idx % 128 // 32])


BF16 = ml_dtypes.bfloat16


def bf(x):
    return np.asarray(x, np.float32).astype(BF16)


def f64(x):
    return np.asarray(x).astype(np.float64)


E2M1 = np.array([0.0, 0.5, 1.0, 1.5, 2.0, 3.0, 4.0, 6.0, -0.0, -0.5, -1.0, -1.5, -2.0, -3.0, -4.0, -6.0])


def pack_weight(w, fmt):
    k, n = w.shape
    w = f64(bf(w)).reshape(k // 32, 32, n)
    amax = np.abs(w).max(1)
    if fmt == "e4m3":
        byte = np.frexp(amax)[1] - 1 + 127 - 7
    else:
        mant, ex = np.frexp(amax / 6.0)
        byte = np.where(mant > 0.5, ex, ex - 1) + 127
    byte = np.clip(np.where(amax > 0, byte, 1), 1, 254)
    scaled = (w * np.exp2(127.0 - byte)[:, None, :]).reshape(k, n).astype(np.float32)
    by_word = np.ascontiguousarray(scaled.reshape(k // 512, 128, 4, n).transpose(0, 1, 3, 2))
    if fmt == "e4m3":
        words = by_word.astype(ml_dtypes.float8_e4m3fn).view(np.uint8)
    else:
        c = by_word.astype(ml_dtypes.float4_e2m1fn).view(np.uint8) & 0xF
        words = c[..., 0::2] | (c[..., 1::2] << 4)
    return np.ascontiguousarray(words), np.ascontiguousarray(byte.astype(np.uint8).reshape(k // 512, 16, n))


def unpack_weight(words, scales, fmt):
    g, p, n, _ = words.shape
    if fmt == "e4m3":
        vals = np.ascontiguousarray(words).view(ml_dtypes.float8_e4m3fn).astype(np.float64)
    else:
        nib = np.empty((g, p, n, 4), np.uint8)
        nib[..., 0::2] = words & 0xF
        nib[..., 1::2] = words >> 4
        vals = E2M1[nib]
    vals = vals * np.repeat(np.exp2(scales.astype(np.float64) - 127.0), 8, axis=1)[..., None]
    return vals.transpose(0, 1, 3, 2).reshape(g * 512, n)

def pack4(w):
    words, scales = pack_weight(w, "e2m1")
    return words.reshape(words.shape[0], 128, -1), scales


def unpack4(words, scales):
    return unpack_weight(words.reshape(words.shape[0], 128, -1, 2), scales, "e2m1")


B, S, D, H, HKV, HD, WINDOW, KB = 1, 128, 512, 16, 8, 128, 256, 512
EPS = 1e-6
THETA = 10000.0


def rope_tables():
    inv_freq = 1.0 / THETA ** (np.arange(0, HD, 2) / HD)
    ang = np.arange(S)[:, None] * inv_freq[None, :]
    emb = np.concatenate([ang, ang], axis=-1)
    return np.broadcast_to(np.cos(emb)[None], (B, S, HD)), np.broadcast_to(np.sin(emb)[None], (B, S, HD))


def rms_norm(x, gain):
    var = np.mean(x * x, axis=-1, keepdims=True)
    return x * (1.0 / np.sqrt(var + EPS)) * gain


def rotate_half(x):
    return np.concatenate([-x[..., HD // 2:], x[..., :HD // 2]], axis=-1)


def apply_rope(x, cos, sin):
    return x * cos[:, :, None, :] + rotate_half(x) * sin[:, :, None, :]


def setup_inputs():
    s = mx_kscale(D)
    cos, sin = rope_tables()
    hidden_states = bf(np.random.standard_normal((B, S, D)) * s)
    Wq_words, Wq_scales = pack4(np.random.standard_normal((D, H * HD)) / np.sqrt(D) / s[:, None])
    Wk_words, Wk_scales = pack4(np.random.standard_normal((D, HKV * HD)) / np.sqrt(D) / s[:, None])
    Wv_words, Wv_scales = pack4(np.random.standard_normal((D, HKV * HD)) * 2.0 / np.sqrt(D) / s[:, None])
    q_scale = bf(np.random.uniform(0.5, 1.5, HD))
    k_scale = bf(np.random.uniform(0.5, 1.5, HD))
    return {
        "hidden_states": hidden_states,
        "cos": bf(cos),
        "sin": bf(sin),
        "Wq_words": Wq_words,
        "Wq_scales": Wq_scales,
        "Wk_words": Wk_words,
        "Wk_scales": Wk_scales,
        "Wv_words": Wv_words,
        "Wv_scales": Wv_scales,
        "q_scale": q_scale,
        "k_scale": k_scale,
    }


def reference(hidden_states, cos, sin, Wq_words, Wq_scales, Wk_words, Wk_scales, Wv_words, Wv_scales, q_scale, k_scale):
    xq = mxq(f64(hidden_states), 2, "e4m3")
    q = (xq @ unpack4(Wq_words, Wq_scales)).reshape(B, S, H, HD)
    k = (xq @ unpack4(Wk_words, Wk_scales)).reshape(B, S, HKV, HD)
    v = (xq @ unpack4(Wv_words, Wv_scales)).reshape(B, S, HKV, HD)
    q = rms_norm(q, f64(q_scale))
    k = rms_norm(k, f64(k_scale))
    q = apply_rope(q, f64(cos), f64(sin))
    k = apply_rope(k, f64(cos), f64(sin))
    return q, k, v

@@ -1,0 +1,240 @@
+from contextlib import ExitStack
+
+import concourse.mybir as mybir
+from concourse.masks import make_identity
+
+F32 = mybir.dt.float32
+BF16 = mybir.dt.bfloat16
+I32 = mybir.dt.int32
+U32 = mybir.dt.uint32
+U8 = mybir.dt.uint8
+FP8X4 = mybir.dt.float8_e4m3fn_x4
+FP4X4 = mybir.dt.float4_e2m1fn_x4
+ACT = mybir.ActivationFunctionType
+ALU = mybir.AluOpType
+
+P = 128
+K = 512
+HEAD = 128
+HALF = HEAD // 2
+BANK = 512
+HEADS_PER_BANK = BANK // HEAD
+Q_COLS, K_COLS, V_COLS = 2048, 1024, 1024
+ROPE_BANKS = (Q_COLS + K_COLS) // BANK
+ALL_BANKS = (Q_COLS + K_COLS + V_COLS) // BANK
+EPS = 1e-6
+SCALE_LAG = 3
+V_STEP = 4
+
+FLOPS = 2 * P * K * (Q_COLS + K_COLS + V_COLS)
+
+
+def tile_multiheadattention_pa_s_kernel(
+    tc,
+    hidden_states,
+    cos,
+    sin,
+    Wq_words,
+    Wq_scales,
+    Wk_words,
+    Wk_scales,
+    Wv_words,
+    Wv_scales,
+    q_scale,
+    k_scale,
+    out_0,
+    out_1,
+    out_2,
+):
+    nc = tc.nc
+    with ExitStack() as ctx:
+        keep = ctx.enter_context(tc.tile_pool(name="keep", bufs=1))
+        work = ctx.enter_context(tc.tile_pool(name="work", bufs=ROPE_BANKS))
+        psum = ctx.enter_context(tc.psum_pool(name="psum", bufs=1))
+        ctx.enter_context(tc.manual_schedule())
+
+        x_sb = keep.tile([P, K], BF16, name="x_sb")
+        x_grouped = keep.tile([P, K], BF16, name="x_grouped", align_bytes=64)
+        x_codes = keep.tile([P, P], U32, name="x_codes", align_bytes=64)
+        x_plane = keep.tile([P, P], U8, name="x_plane", align_bytes=64)
+        identity = keep.tile([P, P], F32, name="identity")
+        ones = keep.tile([P, P], BF16, name="ones")
+        gain_rows = keep.tile([P, 2, HEAD], BF16, name="gain_rows")
+        cos_sb = keep.tile([P, HEAD], BF16, name="cos_sb")
+        sin_sb = keep.tile([P, HEAD], BF16, name="sin_sb")
+        direct_table = keep.tile([P, 2, HEAD], F32, name="direct_table")
+        crossed_table = keep.tile([P, 2, HEAD], F32, name="crossed_table")
+        eps = keep.tile([P, 1], F32, name="eps")
+        table_warmer = keep.tile([P, 1], F32, name="table_warmer")
+        sum_sq = keep.tile([P, ROPE_BANKS * HEADS_PER_BANK], F32, name="sum_sq")
+        inv_rms = keep.tile([P, ROPE_BANKS * HEADS_PER_BANK], F32, name="inv_rms")
+
+        weights = []
+        for label, words, scales, out in (
+            ("q", Wq_words, Wq_scales, out_0),
+            ("k", Wk_words, Wk_scales, out_1),
+            ("v", Wv_words, Wv_scales, out_2),
+        ):
+            cols = scales.shape[2]
+            words_sb = keep.tile([P, 2 * cols], U8, name="words_%s" % label, align_bytes=64)
+            plane_sb = keep.tile([P, cols], U8, name="plane_%s" % label, align_bytes=64)
+            weights.append((words, scales, out, cols, words_sb, plane_sb))
+
+        nc.vector.memset(weights[0][5][:].bitcast(I32), 0)
+        nc.vector.memset(gain_rows[:], 0.0)
+        nc.vector.memset(eps[:], EPS)
+        nc.vector.memset(weights[1][5][:].bitcast(I32), 0)
+        nc.vector.memset(weights[2][5][:].bitcast(I32), 0)
+        nc.vector.memset(ones[:], 1.0)
+        make_identity(nc, identity[:])
+
+        nc.sync.dma_start(out=x_sb[:], in_=hidden_states.flatten_outer_dims())
+        for words, scales, out, cols, words_sb, plane_sb in weights:
+            for r in range(4):
+                nc.sync.dma_start(
+                    out=plane_sb[r:P:32, :].bitcast(I32),
+                    in_=scales.flatten_outer_dims()[r:16:4, :].bitcast(I32),
+                )
+            nc.sync.dma_start(
+                out=words_sb[:].bitcast(I32), in_=words.flatten_outer_dims().bitcast(I32)
+            )
+        nc.scalar.dma_start(out=gain_rows[0:1, 0, :], in_=q_scale.unsqueeze(0))
+        nc.scalar.dma_start(out=gain_rows[0:1, 1, :], in_=k_scale.unsqueeze(0))
+        nc.scalar.dma_start(out=cos_sb[:], in_=cos.flatten_outer_dims())
+        nc.scalar.dma_start(out=sin_sb[:], in_=sin.flatten_outer_dims())
+        nc.scalar.activation(out=table_warmer[:], in_=eps[:], func=ACT.Abs_reciprocal_sqrt)
+
+        x_words = x_sb[:].bitcast(F32)
+        x_pairs = psum.tile([P, 2, P], F32, name="x_pairs", tag="bank%d" % (ALL_BANKS - 1))
+        for u in range(2):
+            nc.tensor.transpose(x_pairs[:, u, :], x_words[:, u : K // 2 : 2], identity[:])
+        nc.vector.tensor_copy(
+            out=x_grouped[:].bitcast(F32).rearrange("p (s u) -> p s u", u=2),
+            in_=x_pairs[:].rearrange("p u s -> p s u"),
+        )
+        nc.vector.quantize_mx(out=x_codes[:].bitcast(FP8X4), scales=x_plane[:], in_=x_grouped[:])
+
+        gains = psum.tile([P, 2, HEAD], F32, name="gains", tag="bank%d" % (ALL_BANKS - 2))
+        nc.tensor.matmul(out=gains[:], lhsT=ones[:], rhs=gain_rows[:], start=True, stop=True)
+        nc.vector.tensor_tensor(
+            out=direct_table[:],
+            in0=gains[:],
+            in1=cos_sb[:].unsqueeze(1).to_broadcast([P, 2, HEAD]),
+            op=ALU.mult,
+        )
+        nc.vector.scalar_tensor_tensor(
+            out=crossed_table[:, :, 0:HALF],
+            in0=gains[:, :, HALF:HEAD],
+            scalar=-1.0,
+            in1=sin_sb[:, 0:HALF].unsqueeze(1).to_broadcast([P, 2, HALF]),
+            op0=ALU.mult,
+            op1=ALU.mult,
+        )
+        nc.vector.tensor_tensor(
+            out=crossed_table[:, :, HALF:HEAD],
+            in0=gains[:, :, 0:HALF],
+            in1=sin_sb[:, HALF:HEAD].unsqueeze(1).to_broadcast([P, 2, HALF]),
+            op=ALU.mult,
+        )
+
+        products = []
+        for which, (words, scales, out, cols, words_sb, plane_sb) in enumerate(weights):
+            out_rows = out.rearrange("b s h d -> (b s) (h d)")
+            for c0 in range(0, cols, BANK):
+                bank = len(products)
+                product = psum.tile([P, BANK], F32, name="product%d" % bank, tag="bank%d" % bank)
+                nc.tensor.matmul_mx(
+                    out=product[:],
+                    lhsT=x_codes[:].bitcast(FP8X4),
+                    lhsT_scale=x_plane[:],
+                    rhs=words_sb[:, 2 * c0 : 2 * (c0 + BANK)].bitcast(FP4X4),
+                    rhs_scale=plane_sb[:, c0 : c0 + BANK],
+                    start=True,
+                    stop=True,
+                )
+                products.append((product, out_rows[:, c0 : c0 + BANK], which))
+
+        rotated_tiles = []
+
+        def sum_squares(bank):
+            product = products[bank][0]
+            squares = work.tile([P, BANK], F32, name="squares")
+            for h in range(HEADS_PER_BANK):
+                head_cols = slice(h * HEAD, (h + 1) * HEAD)
+                head = bank * HEADS_PER_BANK + h
+                nc.scalar.activation(
+                    out=squares[:, head_cols],
+                    in_=product[:, head_cols],
+                    func=ACT.Square,
+                    accum_out=sum_sq[:, head : head + 1],
+                )
+
+        def inverse_rms(bank):
+            heads = slice(bank * HEADS_PER_BANK, (bank + 1) * HEADS_PER_BANK)
+            nc.scalar.activation(
+                out=inv_rms[:, heads],
+                in_=sum_sq[:, heads],
+                func=ACT.Abs_reciprocal_sqrt,
+                scale=1.0 / HEAD,
+                bias=eps[:],
+            )
+
+        def rotate(bank):
+            product, out_cols, which = products[bank]
+            direct = work.tile([P, HEADS_PER_BANK, HEAD], F32, name="direct")
+            crossed = work.tile([P, HEADS_PER_BANK, 2, HALF], F32, name="crossed")
+            rotated = work.tile([P, BANK], F32, name="rotated")
+            rotated_tiles.append(rotated)
+            nc.vector.tensor_tensor(
+                out=direct[:],
+                in0=product[:].rearrange("p (h d) -> p h d", d=HEAD),
+                in1=direct_table[:, which : which + 1, :].to_broadcast([P, HEADS_PER_BANK, HEAD]),
+                op=ALU.mult,
+            )
+            halves = product[:].rearrange("p (h t j) -> p h t j", t=2, j=HALF)
+            for t in range(2):
+                nc.vector.tensor_tensor(
+                    out=crossed[:, :, t, :],
+                    in0=halves[:, :, 1 - t, :],
+                    in1=crossed_table[:, which : which + 1, t * HALF : (t + 1) * HALF].to_broadcast(
+                        [P, HEADS_PER_BANK, HALF]
+                    ),
+                    op=ALU.mult,
+                )
+            adder = nc.gpsimd if bank < ROPE_BANKS - 1 else nc.vector
+            adder.tensor_tensor(
+                out=rotated[:],
+                in0=direct[:].rearrange("p h d -> p (h d)"),
+                in1=crossed[:].rearrange("p h t j -> p (h t j)"),
+                op=ALU.add,
+            )
+
+        def scale_and_store(bank):
+            rotated = rotated_tiles[bank]
+            for h in range(HEADS_PER_BANK):
+                head_cols = slice(h * HEAD, (h + 1) * HEAD)
+                head = bank * HEADS_PER_BANK + h
+                nc.scalar.activation(
+                    out=rotated[:, head_cols],
+                    in_=rotated[:, head_cols],
+                    func=ACT.Copy,
+                    scale=inv_rms[:, head : head + 1],
+                )
+            nc.sync.dma_start(out=products[bank][1], in_=rotated[:])
+
+        def copy_and_store(bank):
+            values = work.tile([P, BANK], F32, name="values")
+            nc.vector.tensor_copy(out=values[:], in_=products[bank][0][:])
+            nc.sync.dma_start(out=products[bank][1], in_=values[:])
+
+        for step in range(ROPE_BANKS + SCALE_LAG):
+            if step < ROPE_BANKS:
+                sum_squares(step)
+                rotate(step)
+            if 1 <= step <= ROPE_BANKS:
+                inverse_rms(step - 1)
+            if step >= SCALE_LAG:
+                scale_and_store(step - SCALE_LAG)
+            if step == V_STEP:
+                for bank in range(ROPE_BANKS, ALL_BANKS):
+                    copy_and_store(bank)

@@ -81,15 +81,15 @@ def tile_multiheadattention_pa_s_kernel(
             weights.append((words, scales, out, cols, words_sb, plane_sb))
 
         nc.vector.memset(weights[0][5][:].bitcast(I32), 0)
-        nc.vector.memset(gain_rows[:], 0.0)
         nc.vector.memset(eps[:], EPS)
         nc.vector.memset(weights[1][5][:].bitcast(I32), 0)
         nc.vector.memset(weights[2][5][:].bitcast(I32), 0)
         nc.vector.memset(ones[:], 1.0)
+        nc.gpsimd.memset(gain_rows[:], 0.0)
         make_identity(nc, identity[:])
 
-        nc.sync.dma_start(out=x_sb[:], in_=hidden_states.flatten_outer_dims())
-        for words, scales, out, cols, words_sb, plane_sb in weights:
+        def load_weight(weight):
+            words, scales, out, cols, words_sb, plane_sb = weight
             for r in range(4):
                 nc.sync.dma_start(
                     out=plane_sb[r:P:32, :].bitcast(I32),
@@ -98,11 +98,16 @@ def tile_multiheadattention_pa_s_kernel(
             nc.sync.dma_start(
                 out=words_sb[:].bitcast(I32), in_=words.flatten_outer_dims().bitcast(I32)
             )
+
         nc.scalar.dma_start(out=gain_rows[0:1, 0, :], in_=q_scale.unsqueeze(0))
         nc.scalar.dma_start(out=gain_rows[0:1, 1, :], in_=k_scale.unsqueeze(0))
+        nc.sync.dma_start(out=x_sb[:], in_=hidden_states.flatten_outer_dims())
+        load_weight(weights[0])
+        nc.scalar.activation(out=table_warmer[:], in_=eps[:], func=ACT.Abs_reciprocal_sqrt)
         nc.scalar.dma_start(out=cos_sb[:], in_=cos.flatten_outer_dims())
         nc.scalar.dma_start(out=sin_sb[:], in_=sin.flatten_outer_dims())
-        nc.scalar.activation(out=table_warmer[:], in_=eps[:], func=ACT.Abs_reciprocal_sqrt)
+        load_weight(weights[1])
+        load_weight(weights[2])
 
         x_words = x_sb[:].bitcast(F32)
         x_pairs = psum.tile([P, 2, P], F32, name="x_pairs", tag="bank%d" % (ALL_BANKS - 1))

@@ -23,8 +23,7 @@ Q_COLS, K_COLS, V_COLS = 2048, 1024, 1024
 ROPE_BANKS = (Q_COLS + K_COLS) // BANK
 ALL_BANKS = (Q_COLS + K_COLS + V_COLS) // BANK
 EPS = 1e-6
-SCALE_LAG = 3
-V_STEP = 4
+V_AFTER = 2
 
 FLOPS = 2 * P * K * (Q_COLS + K_COLS + V_COLS)
 
@@ -62,8 +61,7 @@ def tile_multiheadattention_pa_s_kernel(
         gain_rows = keep.tile([P, 2, HEAD], BF16, name="gain_rows")
         cos_sb = keep.tile([P, HEAD], BF16, name="cos_sb")
         sin_sb = keep.tile([P, HEAD], BF16, name="sin_sb")
-        direct_table = keep.tile([P, 2, HEAD], F32, name="direct_table")
-        crossed_table = keep.tile([P, 2, HEAD], F32, name="crossed_table")
+        tables = keep.tile([P, 2, 2, HEAD], F32, name="tables")
         eps = keep.tile([P, 1], F32, name="eps")
         table_warmer = keep.tile([P, 1], F32, name="table_warmer")
         sum_sq = keep.tile([P, ROPE_BANKS * HEADS_PER_BANK], F32, name="sum_sq")
@@ -121,26 +119,26 @@ def tile_multiheadattention_pa_s_kernel(
 
         gains = psum.tile([P, 2, HEAD], F32, name="gains", tag="bank%d" % (ALL_BANKS - 2))
         nc.tensor.matmul(out=gains[:], lhsT=ones[:], rhs=gain_rows[:], start=True, stop=True)
-        nc.vector.tensor_tensor(
-            out=direct_table[:],
-            in0=gains[:],
-            in1=cos_sb[:].unsqueeze(1).to_broadcast([P, 2, HEAD]),
-            op=ALU.mult,
-        )
-        nc.vector.scalar_tensor_tensor(
-            out=crossed_table[:, :, 0:HALF],
-            in0=gains[:, :, HALF:HEAD],
-            scalar=-1.0,
-            in1=sin_sb[:, 0:HALF].unsqueeze(1).to_broadcast([P, 2, HALF]),
-            op0=ALU.mult,
-            op1=ALU.mult,
-        )
-        nc.vector.tensor_tensor(
-            out=crossed_table[:, :, HALF:HEAD],
-            in0=gains[:, :, 0:HALF],
-            in1=sin_sb[:, HALF:HEAD].unsqueeze(1).to_broadcast([P, 2, HALF]),
-            op=ALU.mult,
-        )
+
+        def make_tables(which):
+            gain = gains[:, which, :]
+            nc.vector.tensor_tensor(
+                out=tables[:, which, 0, :], in0=gain, in1=cos_sb[:], op=ALU.mult
+            )
+            nc.vector.tensor_tensor(
+                out=tables[:, which, 1, 0:HALF],
+                in0=gain[:, 0:HALF],
+                in1=sin_sb[:, HALF:HEAD],
+                op=ALU.mult,
+            )
+            nc.vector.scalar_tensor_tensor(
+                out=tables[:, which, 1, HALF:HEAD],
+                in0=gain[:, HALF:HEAD],
+                scalar=-1.0,
+                in1=sin_sb[:, 0:HALF],
+                op0=ALU.mult,
+                op1=ALU.mult,
+            )
 
         products = []
         for which, (words, scales, out, cols, words_sb, plane_sb) in enumerate(weights):
@@ -159,9 +157,7 @@ def tile_multiheadattention_pa_s_kernel(
                 )
                 products.append((product, out_rows[:, c0 : c0 + BANK], which))
 
-        rotated_tiles = []
-
-        def sum_squares(bank):
+        def inverse_rms(bank):
             product = products[bank][0]
             squares = work.tile([P, BANK], F32, name="squares")
             for h in range(HEADS_PER_BANK):
@@ -173,8 +169,6 @@ def tile_multiheadattention_pa_s_kernel(
                     func=ACT.Square,
                     accum_out=sum_sq[:, head : head + 1],
                 )
-
-        def inverse_rms(bank):
             heads = slice(bank * HEADS_PER_BANK, (bank + 1) * HEADS_PER_BANK)
             nc.scalar.activation(
                 out=inv_rms[:, heads],
@@ -184,62 +178,41 @@ def tile_multiheadattention_pa_s_kernel(
                 bias=eps[:],
             )
 
-        def rotate(bank):
+        def rotate_and_store(bank):
             product, out_cols, which = products[bank]
-            direct = work.tile([P, HEADS_PER_BANK, HEAD], F32, name="direct")
-            crossed = work.tile([P, HEADS_PER_BANK, 2, HALF], F32, name="crossed")
-            rotated = work.tile([P, BANK], F32, name="rotated")
-            rotated_tiles.append(rotated)
-            nc.vector.tensor_tensor(
-                out=direct[:],
-                in0=product[:].rearrange("p (h d) -> p h d", d=HEAD),
-                in1=direct_table[:, which : which + 1, :].to_broadcast([P, HEADS_PER_BANK, HEAD]),
-                op=ALU.mult,
-            )
-            halves = product[:].rearrange("p (h t j) -> p h t j", t=2, j=HALF)
-            for t in range(2):
-                nc.vector.tensor_tensor(
-                    out=crossed[:, :, t, :],
-                    in0=halves[:, :, 1 - t, :],
-                    in1=crossed_table[:, which : which + 1, t * HALF : (t + 1) * HALF].to_broadcast(
-                        [P, HEADS_PER_BANK, HALF]
-                    ),
-                    op=ALU.mult,
+            stay_cross = work.tile([P, HEADS_PER_BANK, 2, 2, HALF], F32, name="stay_cross")
+            rotated = work.tile([P, HEADS_PER_BANK, 2, HALF], F32, name="rotated")
+            for h in range(HEADS_PER_BANK):
+                head = bank * HEADS_PER_BANK + h
+                nc.vector.scalar_tensor_tensor(
+                    out=stay_cross[:, h].rearrange("p w t j -> p w (t j)"),
+                    in0=product[:, h * HEAD : (h + 1) * HEAD].unsqueeze(1).to_broadcast([P, 2, HEAD]),
+                    scalar=inv_rms[:, head : head + 1],
+                    in1=tables[:, which],
+                    op0=ALU.mult,
+                    op1=ALU.mult,
                 )
             adder = nc.gpsimd if bank < ROPE_BANKS - 1 else nc.vector
             adder.tensor_tensor(
                 out=rotated[:],
-                in0=direct[:].rearrange("p h d -> p (h d)"),
-                in1=crossed[:].rearrange("p h t j -> p (h t j)"),
+                in0=stay_cross[:, :, 0, :, :],
+                in1=stay_cross[:, :, 1, ::-1, :],
                 op=ALU.add,
             )
-
-        def scale_and_store(bank):
-            rotated = rotated_tiles[bank]
-            for h in range(HEADS_PER_BANK):
-                head_cols = slice(h * HEAD, (h + 1) * HEAD)
-                head = bank * HEADS_PER_BANK + h
-                nc.scalar.activation(
-                    out=rotated[:, head_cols],
-                    in_=rotated[:, head_cols],
-                    func=ACT.Copy,
-                    scale=inv_rms[:, head : head + 1],
-                )
-            nc.sync.dma_start(out=products[bank][1], in_=rotated[:])
+            nc.sync.dma_start(out=out_cols, in_=rotated[:].rearrange("p h t j -> p (h t j)"))
 
         def copy_and_store(bank):
             values = work.tile([P, BANK], F32, name="values")
-            nc.vector.tensor_copy(out=values[:], in_=products[bank][0][:])
+            nc.scalar.copy(out=values[:], in_=products[bank][0][:])
             nc.sync.dma_start(out=products[bank][1], in_=values[:])
 
-        for step in range(ROPE_BANKS + SCALE_LAG):
-            if step < ROPE_BANKS:
-                sum_squares(step)
-                rotate(step)
-            if 1 <= step <= ROPE_BANKS:
-                inverse_rms(step - 1)
-            if step >= SCALE_LAG:
-                scale_and_store(step - SCALE_LAG)
-            if step == V_STEP:
-                for bank in range(ROPE_BANKS, ALL_BANKS):
-                    copy_and_store(bank)
+        for bank in range(ROPE_BANKS):
+            inverse_rms(bank)
+        make_tables(0)
+        for bank in range(ROPE_BANKS):
+            rotate_and_store(bank)
+            if bank == 0:
+                make_tables(1)
+            if bank == V_AFTER:
+                for v_bank in range(ROPE_BANKS, ALL_BANKS):
+                    copy_and_store(v_bank)

@@ -119,26 +119,26 @@ def tile_multiheadattention_pa_s_kernel(
 
         gains = psum.tile([P, 2, HEAD], F32, name="gains", tag="bank%d" % (ALL_BANKS - 2))
         nc.tensor.matmul(out=gains[:], lhsT=ones[:], rhs=gain_rows[:], start=True, stop=True)
-
-        def make_tables(which):
-            gain = gains[:, which, :]
-            nc.vector.tensor_tensor(
-                out=tables[:, which, 0, :], in0=gain, in1=cos_sb[:], op=ALU.mult
-            )
-            nc.vector.tensor_tensor(
-                out=tables[:, which, 1, 0:HALF],
-                in0=gain[:, 0:HALF],
-                in1=sin_sb[:, HALF:HEAD],
-                op=ALU.mult,
-            )
-            nc.vector.scalar_tensor_tensor(
-                out=tables[:, which, 1, HALF:HEAD],
-                in0=gain[:, HALF:HEAD],
-                scalar=-1.0,
-                in1=sin_sb[:, 0:HALF],
-                op0=ALU.mult,
-                op1=ALU.mult,
-            )
+        nc.vector.tensor_tensor(
+            out=tables[:, :, 0, :],
+            in0=gains[:],
+            in1=cos_sb[:].unsqueeze(1).to_broadcast([P, 2, HEAD]),
+            op=ALU.mult,
+        )
+        nc.vector.tensor_tensor(
+            out=tables[:, :, 1, 0:HALF],
+            in0=gains[:, :, 0:HALF],
+            in1=sin_sb[:, HALF:HEAD].unsqueeze(1).to_broadcast([P, 2, HALF]),
+            op=ALU.mult,
+        )
+        nc.vector.scalar_tensor_tensor(
+            out=tables[:, :, 1, HALF:HEAD],
+            in0=gains[:, :, HALF:HEAD],
+            scalar=-1.0,
+            in1=sin_sb[:, 0:HALF].unsqueeze(1).to_broadcast([P, 2, HALF]),
+            op0=ALU.mult,
+            op1=ALU.mult,
+        )
 
         products = []
         for which, (words, scales, out, cols, words_sb, plane_sb) in enumerate(weights):
@@ -208,11 +208,8 @@ def tile_multiheadattention_pa_s_kernel(
 
         for bank in range(ROPE_BANKS):
             inverse_rms(bank)
-        make_tables(0)
         for bank in range(ROPE_BANKS):
             rotate_and_store(bank)
-            if bank == 0:
-                make_tables(1)
             if bank == V_AFTER:
                 for v_bank in range(ROPE_BANKS, ALL_BANKS):
                     copy_and_store(v_bank)

@@ -20,10 +20,11 @@ HALF = HEAD // 2
 BANK = 512
 HEADS_PER_BANK = BANK // HEAD
 Q_COLS, K_COLS, V_COLS = 2048, 1024, 1024
-ROPE_BANKS = (Q_COLS + K_COLS) // BANK
+ROPE_HEADS = (Q_COLS + K_COLS) // HEAD
+ROPE_UNITS = ROPE_HEADS // HEADS_PER_BANK
 ALL_BANKS = (Q_COLS + K_COLS + V_COLS) // BANK
 EPS = 1e-6
-V_AFTER = 2
+GROUP_HEADS = (1, 1, 2, 4, 4, 4, 4, 4)
 
 FLOPS = 2 * P * K * (Q_COLS + K_COLS + V_COLS)
 
@@ -48,7 +49,7 @@ def tile_multiheadattention_pa_s_kernel(
     nc = tc.nc
     with ExitStack() as ctx:
         keep = ctx.enter_context(tc.tile_pool(name="keep", bufs=1))
-        work = ctx.enter_context(tc.tile_pool(name="work", bufs=ROPE_BANKS))
+        work = ctx.enter_context(tc.tile_pool(name="work", bufs=ALL_BANKS))
         psum = ctx.enter_context(tc.psum_pool(name="psum", bufs=1))
         ctx.enter_context(tc.manual_schedule())
 
@@ -64,8 +65,9 @@ def tile_multiheadattention_pa_s_kernel(
         tables = keep.tile([P, 2, 2, HEAD], F32, name="tables")
         eps = keep.tile([P, 1], F32, name="eps")
         table_warmer = keep.tile([P, 1], F32, name="table_warmer")
-        sum_sq = keep.tile([P, ROPE_BANKS * HEADS_PER_BANK], F32, name="sum_sq")
-        inv_rms = keep.tile([P, ROPE_BANKS * HEADS_PER_BANK], F32, name="inv_rms")
+        sum_sq = keep.tile([P, ROPE_HEADS], F32, name="sum_sq")
+        inv_rms = keep.tile([P, ROPE_HEADS], F32, name="inv_rms")
+        values = keep.tile([P, V_COLS], F32, name="values")
 
         weights = []
         for label, words, scales, out in (
@@ -140,59 +142,66 @@ def tile_multiheadattention_pa_s_kernel(
             op1=ALU.mult,
         )
 
-        products = []
-        for which, (words, scales, out, cols, words_sb, plane_sb) in enumerate(weights):
-            out_rows = out.rearrange("b s h d -> (b s) (h d)")
-            for c0 in range(0, cols, BANK):
-                bank = len(products)
-                product = psum.tile([P, BANK], F32, name="product%d" % bank, tag="bank%d" % bank)
-                nc.tensor.matmul_mx(
-                    out=product[:],
-                    lhsT=x_codes[:].bitcast(FP8X4),
-                    lhsT_scale=x_plane[:],
-                    rhs=words_sb[:, 2 * c0 : 2 * (c0 + BANK)].bitcast(FP4X4),
-                    rhs_scale=plane_sb[:, c0 : c0 + BANK],
-                    start=True,
-                    stop=True,
-                )
-                products.append((product, out_rows[:, c0 : c0 + BANK], which))
+        def multiply(which, c0, cols, product, p0):
+            words, scales, out, all_cols, words_sb, plane_sb = weights[which]
+            nc.tensor.matmul_mx(
+                out=product[:, p0 : p0 + cols],
+                lhsT=x_codes[:].bitcast(FP8X4),
+                lhsT_scale=x_plane[:],
+                rhs=words_sb[:, 2 * c0 : 2 * (c0 + cols)].bitcast(FP4X4),
+                rhs_scale=plane_sb[:, c0 : c0 + cols],
+                start=True,
+                stop=True,
+            )
 
-        def inverse_rms(bank):
-            product = products[bank][0]
+        banks = []
+        place = []
+        for g, heads in enumerate(GROUP_HEADS):
+            product = psum.tile([P, BANK], F32, name="product%d" % g, tag="bank%d" % g)
+            banks.append(product)
+            first = len(place)
+            for h in range(heads):
+                place.append((g, h * HEAD))
+            which = 0 if first * HEAD < Q_COLS else 1
+            multiply(which, first * HEAD - which * Q_COLS, heads * HEAD, product, 0)
+
+        def inverse_rms(g):
+            heads = [h for h in range(ROPE_HEADS) if place[h][0] == g]
             squares = work.tile([P, BANK], F32, name="squares")
-            for h in range(HEADS_PER_BANK):
-                head_cols = slice(h * HEAD, (h + 1) * HEAD)
-                head = bank * HEADS_PER_BANK + h
+            for head in heads:
+                p0 = place[head][1]
                 nc.scalar.activation(
-                    out=squares[:, head_cols],
-                    in_=product[:, head_cols],
+                    out=squares[:, p0 : p0 + HEAD],
+                    in_=banks[g][:, p0 : p0 + HEAD],
                     func=ACT.Square,
                     accum_out=sum_sq[:, head : head + 1],
                 )
-            heads = slice(bank * HEADS_PER_BANK, (bank + 1) * HEADS_PER_BANK)
             nc.scalar.activation(
-                out=inv_rms[:, heads],
-                in_=sum_sq[:, heads],
+                out=inv_rms[:, heads[0] : heads[-1] + 1],
+                in_=sum_sq[:, heads[0] : heads[-1] + 1],
                 func=ACT.Abs_reciprocal_sqrt,
                 scale=1.0 / HEAD,
                 bias=eps[:],
             )
 
-        def rotate_and_store(bank):
-            product, out_cols, which = products[bank]
+        def rotate_and_store(unit):
+            which = 0 if unit * BANK < Q_COLS else 1
+            c0 = unit * BANK - which * Q_COLS
+            out_cols = weights[which][2].rearrange("b s h d -> (b s) (h d)")[:, c0 : c0 + BANK]
             stay_cross = work.tile([P, HEADS_PER_BANK, 2, 2, HALF], F32, name="stay_cross")
             rotated = work.tile([P, HEADS_PER_BANK, 2, HALF], F32, name="rotated")
             for h in range(HEADS_PER_BANK):
-                head = bank * HEADS_PER_BANK + h
+                head = unit * HEADS_PER_BANK + h
+                g, p0 = place[head]
                 nc.vector.scalar_tensor_tensor(
                     out=stay_cross[:, h].rearrange("p w t j -> p w (t j)"),
-                    in0=product[:, h * HEAD : (h + 1) * HEAD].unsqueeze(1).to_broadcast([P, 2, HEAD]),
+                    in0=banks[g][:, p0 : p0 + HEAD].unsqueeze(1).to_broadcast([P, 2, HEAD]),
                     scalar=inv_rms[:, head : head + 1],
                     in1=tables[:, which],
                     op0=ALU.mult,
                     op1=ALU.mult,
                 )
-            adder = nc.gpsimd if bank < ROPE_BANKS - 1 else nc.vector
+            adder = nc.gpsimd if unit < ROPE_UNITS - 1 else nc.vector
             adder.tensor_tensor(
                 out=rotated[:],
                 in0=stay_cross[:, :, 0, :, :],
@@ -201,15 +210,29 @@ def tile_multiheadattention_pa_s_kernel(
             )
             nc.sync.dma_start(out=out_cols, in_=rotated[:].rearrange("p h t j -> p (h t j)"))
 
-        def copy_and_store(bank):
-            values = work.tile([P, BANK], F32, name="values")
-            nc.scalar.copy(out=values[:], in_=products[bank][0][:])
-            nc.sync.dma_start(out=products[bank][1], in_=values[:])
+        def multiply_v():
+            filled = []
+            c0 = 0
+            for g, heads in enumerate(GROUP_HEADS):
+                p0 = heads * HEAD
+                if p0 < BANK:
+                    filled.append((g, p0, BANK - p0, c0))
+                while p0 < BANK:
+                    cols = min(2 * HEAD, BANK - p0)
+                    multiply(2, c0, cols, banks[g], p0)
+                    p0 += cols
+                    c0 += cols
+            return filled
 
-        for bank in range(ROPE_BANKS):
-            inverse_rms(bank)
-        for bank in range(ROPE_BANKS):
-            rotate_and_store(bank)
-            if bank == V_AFTER:
-                for v_bank in range(ROPE_BANKS, ALL_BANKS):
-                    copy_and_store(v_bank)
+        def copy_and_store_v(filled):
+            out_rows = weights[2][2].rearrange("b s h d -> (b s) (h d)")
+            for g, p0, cols, c0 in filled:
+                nc.scalar.copy(out=values[:, c0 : c0 + cols], in_=banks[g][:, p0 : p0 + cols])
+                nc.scalar.dma_start(out=out_rows[:, c0 : c0 + cols], in_=values[:, c0 : c0 + cols])
+
+        for g in range(ALL_BANKS):
+            inverse_rms(g)
+        for unit in range(ROPE_UNITS):
+            rotate_and_store(unit)
+            if unit == 0:
+                copy_and_store_v(multiply_v())

@@ -24,6 +24,7 @@ ROPE_HEADS = (Q_COLS + K_COLS) // HEAD
 ROPE_UNITS = ROPE_HEADS // HEADS_PER_BANK
 ALL_BANKS = (Q_COLS + K_COLS + V_COLS) // BANK
 EPS = 1e-6
+V_AFTER = 2
 GROUP_HEADS = (1, 1, 2, 4, 4, 4, 4, 4)
 
 FLOPS = 2 * P * K * (Q_COLS + K_COLS + V_COLS)
@@ -228,11 +229,13 @@ def tile_multiheadattention_pa_s_kernel(
             out_rows = weights[2][2].rearrange("b s h d -> (b s) (h d)")
             for g, p0, cols, c0 in filled:
                 nc.scalar.copy(out=values[:, c0 : c0 + cols], in_=banks[g][:, p0 : p0 + cols])
-                nc.scalar.dma_start(out=out_rows[:, c0 : c0 + cols], in_=values[:, c0 : c0 + cols])
+                nc.sync.dma_start(out=out_rows[:, c0 : c0 + cols], in_=values[:, c0 : c0 + cols])
 
         for g in range(ALL_BANKS):
             inverse_rms(g)
         for unit in range(ROPE_UNITS):
             rotate_and_store(unit)
             if unit == 0:
-                copy_and_store_v(multiply_v())
+                filled = multiply_v()
+            if unit == V_AFTER:
+                copy_and_store_v(filled)

@@ -105,8 +105,8 @@ def tile_multiheadattention_pa_s_kernel(
         nc.sync.dma_start(out=x_sb[:], in_=hidden_states.flatten_outer_dims())
         load_weight(weights[0])
         nc.scalar.activation(out=table_warmer[:], in_=eps[:], func=ACT.Abs_reciprocal_sqrt)
-        nc.scalar.dma_start(out=cos_sb[:], in_=cos.flatten_outer_dims())
-        nc.scalar.dma_start(out=sin_sb[:], in_=sin.flatten_outer_dims())
+        nc.sync.dma_start(out=cos_sb[:], in_=cos.flatten_outer_dims())
+        nc.sync.dma_start(out=sin_sb[:], in_=sin.flatten_outer_dims())
         load_weight(weights[1])
         load_weight(weights[2])
 

@@ -166,17 +166,19 @@ def tile_multiheadattention_pa_s_kernel(
             which = 0 if first * HEAD < Q_COLS else 1
             multiply(which, first * HEAD - which * Q_COLS, heads * HEAD, product, 0)
 
+        squares = keep.tile([P, ROPE_HEADS * HEAD], F32, name="squares")
+
+        def sum_squares(head):
+            g, p0 = place[head]
+            nc.scalar.activation(
+                out=squares[:, head * HEAD : (head + 1) * HEAD],
+                in_=banks[g][:, p0 : p0 + HEAD],
+                func=ACT.Square,
+                accum_out=sum_sq[:, head : head + 1],
+            )
+
         def inverse_rms(g):
             heads = [h for h in range(ROPE_HEADS) if place[h][0] == g]
-            squares = work.tile([P, BANK], F32, name="squares")
-            for head in heads:
-                p0 = place[head][1]
-                nc.scalar.activation(
-                    out=squares[:, p0 : p0 + HEAD],
-                    in_=banks[g][:, p0 : p0 + HEAD],
-                    func=ACT.Square,
-                    accum_out=sum_sq[:, head : head + 1],
-                )
             nc.scalar.activation(
                 out=inv_rms[:, heads[0] : heads[-1] + 1],
                 in_=sum_sq[:, heads[0] : heads[-1] + 1],
@@ -231,8 +233,15 @@ def tile_multiheadattention_pa_s_kernel(
                 nc.scalar.copy(out=values[:, c0 : c0 + cols], in_=banks[g][:, p0 : p0 + cols])
                 nc.sync.dma_start(out=out_rows[:, c0 : c0 + cols], in_=values[:, c0 : c0 + cols])
 
-        for g in range(ALL_BANKS):
-            inverse_rms(g)
+        owed = None
+        for head in range(ROPE_HEADS):
+            sum_squares(head)
+            if owed is not None:
+                inverse_rms(owed)
+                owed = None
+            if head + 1 == ROPE_HEADS or place[head + 1][0] != place[head][0]:
+                owed = place[head][0]
+        inverse_rms(owed)
         for unit in range(ROPE_UNITS):
             rotate_and_store(unit)
             if unit == 0:

@@ -89,26 +89,31 @@ def tile_multiheadattention_pa_s_kernel(
         nc.gpsimd.memset(gain_rows[:], 0.0)
         make_identity(nc, identity[:])
 
-        def load_weight(weight):
+        def load_weight(weight, words_first):
             words, scales, out, cols, words_sb, plane_sb = weight
+            if words_first:
+                nc.sync.dma_start(
+                    out=words_sb[:].bitcast(I32), in_=words.flatten_outer_dims().bitcast(I32)
+                )
             for r in range(4):
                 nc.sync.dma_start(
                     out=plane_sb[r:P:32, :].bitcast(I32),
                     in_=scales.flatten_outer_dims()[r:16:4, :].bitcast(I32),
                 )
-            nc.sync.dma_start(
-                out=words_sb[:].bitcast(I32), in_=words.flatten_outer_dims().bitcast(I32)
-            )
+            if not words_first:
+                nc.sync.dma_start(
+                    out=words_sb[:].bitcast(I32), in_=words.flatten_outer_dims().bitcast(I32)
+                )
 
         nc.scalar.dma_start(out=gain_rows[0:1, 0, :], in_=q_scale.unsqueeze(0))
         nc.scalar.dma_start(out=gain_rows[0:1, 1, :], in_=k_scale.unsqueeze(0))
         nc.sync.dma_start(out=x_sb[:], in_=hidden_states.flatten_outer_dims())
-        load_weight(weights[0])
+        load_weight(weights[0], True)
         nc.scalar.activation(out=table_warmer[:], in_=eps[:], func=ACT.Abs_reciprocal_sqrt)
         nc.sync.dma_start(out=cos_sb[:], in_=cos.flatten_outer_dims())
         nc.sync.dma_start(out=sin_sb[:], in_=sin.flatten_outer_dims())
-        load_weight(weights[1])
-        load_weight(weights[2])
+        load_weight(weights[1], False)
+        load_weight(weights[2], False)
 
         x_words = x_sb[:].bitcast(F32)
         x_pairs = psum.tile([P, 2, P], F32, name="x_pairs", tag="bank%d" % (ALL_BANKS - 1))

@@ -192,7 +192,7 @@ def tile_multiheadattention_pa_s_kernel(
                 bias=eps[:],
             )
 
-        def rotate_and_store(unit):
+        def multiply_by_tables(unit):
             which = 0 if unit * BANK < Q_COLS else 1
             c0 = unit * BANK - which * Q_COLS
             out_cols = weights[which][2].rearrange("b s h d -> (b s) (h d)")[:, c0 : c0 + BANK]
@@ -209,13 +209,19 @@ def tile_multiheadattention_pa_s_kernel(
                     op0=ALU.mult,
                     op1=ALU.mult,
                 )
-            adder = nc.gpsimd if unit < ROPE_UNITS - 1 else nc.vector
-            adder.tensor_tensor(
-                out=rotated[:],
-                in0=stay_cross[:, :, 0, :, :],
-                in1=stay_cross[:, :, 1, ::-1, :],
+            return stay_cross, rotated, out_cols
+
+        def add(engine, unit, h0, h1):
+            stay_cross, rotated, out_cols = parts[unit]
+            engine.tensor_tensor(
+                out=rotated[:, h0:h1],
+                in0=stay_cross[:, h0:h1, 0, :, :],
+                in1=stay_cross[:, h0:h1, 1, ::-1, :],
                 op=ALU.add,
             )
+
+        def store(unit):
+            stay_cross, rotated, out_cols = parts[unit]
             nc.sync.dma_start(out=out_cols, in_=rotated[:].rearrange("p h t j -> p (h t j)"))
 
         def multiply_v():
@@ -247,9 +253,20 @@ def tile_multiheadattention_pa_s_kernel(
             if head + 1 == ROPE_HEADS or place[head + 1][0] != place[head][0]:
                 owed = place[head][0]
         inverse_rms(owed)
+        parts = []
         for unit in range(ROPE_UNITS):
-            rotate_and_store(unit)
+            parts.append(multiply_by_tables(unit))
+            if unit < ROPE_UNITS - 2:
+                add(nc.gpsimd, unit, 0, HEADS_PER_BANK)
+                store(unit)
             if unit == 0:
                 filled = multiply_v()
             if unit == V_AFTER:
                 copy_and_store_v(filled)
+        before_last, last = ROPE_UNITS - 2, ROPE_UNITS - 1
+        add(nc.gpsimd, before_last, 0, 2)
+        add(nc.vector, before_last, 2, HEADS_PER_BANK)
+        store(before_last)
+        add(nc.vector, last, 0, 2)
+        add(nc.vector, last, 2, HEADS_PER_BANK)
+        store(last)

@@ -256,7 +256,11 @@ def tile_multiheadattention_pa_s_kernel(
         parts = []
         for unit in range(ROPE_UNITS):
             parts.append(multiply_by_tables(unit))
-            if unit < ROPE_UNITS - 2:
+            if unit == 0:
+                add(nc.gpsimd, unit, 0, 2)
+                add(nc.gpsimd, unit, 2, HEADS_PER_BANK)
+                store(unit)
+            elif unit < ROPE_UNITS - 2:
                 add(nc.gpsimd, unit, 0, HEADS_PER_BANK)
                 store(unit)
             if unit == 0:

@@ -25,7 +25,7 @@ ROPE_UNITS = ROPE_HEADS // HEADS_PER_BANK
 ALL_BANKS = (Q_COLS + K_COLS + V_COLS) // BANK
 EPS = 1e-6
 V_AFTER = 2
-GROUP_HEADS = (1, 1, 2, 4, 4, 4, 4, 4)
+GROUP_HEADS = (1, 2, 2, 3, 4, 4, 4, 4)
 
 FLOPS = 2 * P * K * (Q_COLS + K_COLS + V_COLS)
 
@@ -60,7 +60,9 @@ def tile_multiheadattention_pa_s_kernel(
         x_plane = keep.tile([P, P], U8, name="x_plane", align_bytes=64)
         identity = keep.tile([P, P], F32, name="identity")
         ones = keep.tile([P, P], BF16, name="ones")
+        minus_ones = keep.tile([P, P], BF16, name="minus_ones")
         gain_rows = keep.tile([P, 2, HEAD], BF16, name="gain_rows")
+        k_gains = keep.tile([P, 2, HEAD], F32, name="k_gains")
         cos_sb = keep.tile([P, HEAD], BF16, name="cos_sb")
         sin_sb = keep.tile([P, HEAD], BF16, name="sin_sb")
         tables = keep.tile([P, 2, 2, HEAD], F32, name="tables")
@@ -81,12 +83,13 @@ def tile_multiheadattention_pa_s_kernel(
             plane_sb = keep.tile([P, cols], U8, name="plane_%s" % label, align_bytes=64)
             weights.append((words, scales, out, cols, words_sb, plane_sb))
 
+        nc.vector.memset(gain_rows[:], 0.0)
         nc.vector.memset(weights[0][5][:].bitcast(I32), 0)
         nc.vector.memset(eps[:], EPS)
         nc.vector.memset(weights[1][5][:].bitcast(I32), 0)
         nc.vector.memset(weights[2][5][:].bitcast(I32), 0)
         nc.vector.memset(ones[:], 1.0)
-        nc.gpsimd.memset(gain_rows[:], 0.0)
+        nc.vector.memset(minus_ones[:], -1.0)
         make_identity(nc, identity[:])
 
         def load_weight(weight, words_first):
@@ -125,28 +128,28 @@ def tile_multiheadattention_pa_s_kernel(
         )
         nc.vector.quantize_mx(out=x_codes[:].bitcast(FP8X4), scales=x_plane[:], in_=x_grouped[:])
 
-        gains = psum.tile([P, 2, HEAD], F32, name="gains", tag="bank%d" % (ALL_BANKS - 2))
-        nc.tensor.matmul(out=gains[:], lhsT=ones[:], rhs=gain_rows[:], start=True, stop=True)
-        nc.vector.tensor_tensor(
-            out=tables[:, :, 0, :],
-            in0=gains[:],
-            in1=cos_sb[:].unsqueeze(1).to_broadcast([P, 2, HEAD]),
-            op=ALU.mult,
-        )
-        nc.vector.tensor_tensor(
-            out=tables[:, :, 1, 0:HALF],
-            in0=gains[:, :, 0:HALF],
-            in1=sin_sb[:, HALF:HEAD].unsqueeze(1).to_broadcast([P, 2, HALF]),
-            op=ALU.mult,
-        )
-        nc.vector.scalar_tensor_tensor(
-            out=tables[:, :, 1, HALF:HEAD],
-            in0=gains[:, :, HALF:HEAD],
-            scalar=-1.0,
-            in1=sin_sb[:, 0:HALF].unsqueeze(1).to_broadcast([P, 2, HALF]),
-            op0=ALU.mult,
-            op1=ALU.mult,
-        )
+        gains = psum.tile([P, 2, 2, HEAD], F32, name="gains", tag="bank%d" % (ALL_BANKS - 2))
+        for signs, out, row in (
+            (ones, gains[:, :, 0, :], gain_rows[:]),
+            (ones, gains[:, :, 1, 0:HALF], gain_rows[:, :, 0:HALF]),
+            (minus_ones, gains[:, :, 1, HALF:HEAD], gain_rows[:, :, HALF:HEAD]),
+        ):
+            nc.tensor.matmul(out=out, lhsT=signs[:], rhs=row, start=True, stop=True)
+        nc.scalar.copy(out=k_gains[:], in_=gains[:, 1])
+
+        def make_tables(engine, w, signed_gains):
+            engine.tensor_tensor(
+                out=tables[:, w, 0, :], in0=signed_gains[:, 0, :], in1=cos_sb[:], op=ALU.mult
+            )
+            engine.tensor_tensor(
+                out=tables[:, w, 1, :].rearrange("p (t j) -> p t j", t=2),
+                in0=signed_gains[:, 1, :].rearrange("p (t j) -> p t j", t=2),
+                in1=sin_sb[:].rearrange("p (t j) -> p t j", t=2)[:, ::-1, :],
+                op=ALU.mult,
+            )
+
+        make_tables(nc.vector, 0, gains[:, 0])
+        make_tables(nc.gpsimd, 1, k_gains)
 
         def multiply(which, c0, cols, product, p0):
             words, scales, out, all_cols, words_sb, plane_sb = weights[which]
@@ -160,6 +163,12 @@ def tile_multiheadattention_pa_s_kernel(
                 stop=True,
             )
 
+        def multiply_heads(which, first, heads, product, p0):
+            while heads > 0:
+                n = 4 if heads == 4 else min(heads, 2)
+                multiply(which, first * HEAD, n * HEAD, product, p0)
+                first, heads, p0 = first + n, heads - n, p0 + n * HEAD
+
         banks = []
         place = []
         for g, heads in enumerate(GROUP_HEADS):
@@ -169,7 +178,7 @@ def tile_multiheadattention_pa_s_kernel(
             for h in range(heads):
                 place.append((g, h * HEAD))
             which = 0 if first * HEAD < Q_COLS else 1
-            multiply(which, first * HEAD - which * Q_COLS, heads * HEAD, product, 0)
+            multiply_heads(which, first - which * (Q_COLS // HEAD), heads, product, 0)
 
         squares = keep.tile([P, ROPE_HEADS * HEAD], F32, name="squares")
 
@@ -226,16 +235,13 @@ def tile_multiheadattention_pa_s_kernel(
 
         def multiply_v():
             filled = []
-            c0 = 0
+            first = 0
             for g, heads in enumerate(GROUP_HEADS):
-                p0 = heads * HEAD
-                if p0 < BANK:
-                    filled.append((g, p0, BANK - p0, c0))
-                while p0 < BANK:
-                    cols = min(2 * HEAD, BANK - p0)
-                    multiply(2, c0, cols, banks[g], p0)
-                    p0 += cols
-                    c0 += cols
+                free = HEADS_PER_BANK - heads
+                if free > 0:
+                    filled.append((g, heads * HEAD, free * HEAD, first * HEAD))
+                    multiply_heads(2, first, free, banks[g], heads * HEAD)
+                    first += free
             return filled
 
         def copy_and_store_v(filled):
@@ -263,7 +269,7 @@ def tile_multiheadattention_pa_s_kernel(
             elif unit < ROPE_UNITS - 2:
                 add(nc.gpsimd, unit, 0, HEADS_PER_BANK)
                 store(unit)
-            if unit == 0:
+            if unit == 1:
                 filled = multiply_v()
             if unit == V_AFTER:
                 copy_and_store_v(filled)

@@ -24,8 +24,10 @@ ROPE_HEADS = (Q_COLS + K_COLS) // HEAD
 ROPE_UNITS = ROPE_HEADS // HEADS_PER_BANK
 ALL_BANKS = (Q_COLS + K_COLS + V_COLS) // BANK
 EPS = 1e-6
-V_AFTER = 2
+V_STRETCHES = {2: (0, 1), 3: (1, 2), 4: (2, 4)}
 GROUP_HEADS = (1, 2, 2, 3, 4, 4, 4, 4)
+V_BANKS = 4
+Q_BANKS = 6
 
 FLOPS = 2 * P * K * (Q_COLS + K_COLS + V_COLS)
 
@@ -115,8 +117,8 @@ def tile_multiheadattention_pa_s_kernel(
         nc.scalar.activation(out=table_warmer[:], in_=eps[:], func=ACT.Abs_reciprocal_sqrt)
         nc.sync.dma_start(out=cos_sb[:], in_=cos.flatten_outer_dims())
         nc.sync.dma_start(out=sin_sb[:], in_=sin.flatten_outer_dims())
-        load_weight(weights[1], False)
         load_weight(weights[2], False)
+        load_weight(weights[1], False)
 
         x_words = x_sb[:].bitcast(F32)
         x_pairs = psum.tile([P, 2, P], F32, name="x_pairs", tag="bank%d" % (ALL_BANKS - 1))
@@ -172,13 +174,18 @@ def tile_multiheadattention_pa_s_kernel(
         banks = []
         place = []
         for g, heads in enumerate(GROUP_HEADS):
-            product = psum.tile([P, BANK], F32, name="product%d" % g, tag="bank%d" % g)
-            banks.append(product)
-            first = len(place)
             for h in range(heads):
                 place.append((g, h * HEAD))
+
+        def multiply_bank(g):
+            first = sum(GROUP_HEADS[:g])
+            product = psum.tile([P, BANK], F32, name="product%d" % g, tag="bank%d" % g)
+            banks.append(product)
             which = 0 if first * HEAD < Q_COLS else 1
-            multiply_heads(which, first - which * (Q_COLS // HEAD), heads, product, 0)
+            multiply_heads(which, first - which * (Q_COLS // HEAD), GROUP_HEADS[g], product, 0)
+
+        for g in range(Q_BANKS):
+            multiply_bank(g)
 
         squares = keep.tile([P, ROPE_HEADS * HEAD], F32, name="squares")
 
@@ -229,54 +236,65 @@ def tile_multiheadattention_pa_s_kernel(
                 op=ALU.add,
             )
 
-        def store(unit):
+        def store(unit, h0, h1):
             stay_cross, rotated, out_cols = parts[unit]
-            nc.sync.dma_start(out=out_cols, in_=rotated[:].rearrange("p h t j -> p (h t j)"))
+            nc.sync.dma_start(
+                out=out_cols[:, h0 * HEAD : h1 * HEAD],
+                in_=rotated[:, h0:h1].rearrange("p h t j -> p (h t j)"),
+            )
 
-        def multiply_v():
-            filled = []
-            first = 0
-            for g, heads in enumerate(GROUP_HEADS):
-                free = HEADS_PER_BANK - heads
-                if free > 0:
-                    filled.append((g, heads * HEAD, free * HEAD, first * HEAD))
-                    multiply_heads(2, first, free, banks[g], heads * HEAD)
-                    first += free
-            return filled
+        filled = []
 
-        def copy_and_store_v(filled):
+        def multiply_v(g):
+            free = HEADS_PER_BANK - GROUP_HEADS[g]
+            first = sum(HEADS_PER_BANK - heads for heads in GROUP_HEADS[:g])
+            filled.append((g, GROUP_HEADS[g] * HEAD, free * HEAD, first * HEAD))
+            multiply_heads(2, first, free, banks[g], GROUP_HEADS[g] * HEAD)
+
+        def copy_and_store_v(stretches):
             out_rows = weights[2][2].rearrange("b s h d -> (b s) (h d)")
-            for g, p0, cols, c0 in filled:
+            for g, p0, cols, c0 in stretches:
                 nc.scalar.copy(out=values[:, c0 : c0 + cols], in_=banks[g][:, p0 : p0 + cols])
-                nc.sync.dma_start(out=out_rows[:, c0 : c0 + cols], in_=values[:, c0 : c0 + cols])
+            start, stop = stretches[0][3], stretches[-1][3] + stretches[-1][2]
+            nc.sync.dma_start(out=out_rows[:, start:stop], in_=values[:, start:stop])
 
-        owed = None
-        for head in range(ROPE_HEADS):
-            sum_squares(head)
-            if owed is not None:
-                inverse_rms(owed)
-                owed = None
-            if head + 1 == ROPE_HEADS or place[head + 1][0] != place[head][0]:
-                owed = place[head][0]
-        inverse_rms(owed)
+        squared = 0
+
+        def square_through(unit, squared):
+            last_bank = place[unit * HEADS_PER_BANK + HEADS_PER_BANK - 1][0]
+            stop = sum(GROUP_HEADS[: last_bank + 1])
+            for head in range(squared, min(stop + 1, ROPE_HEADS)):
+                sum_squares(head)
+                if head > 0 and place[head][0] != place[head - 1][0]:
+                    inverse_rms(place[head - 1][0])
+            if stop == ROPE_HEADS:
+                inverse_rms(last_bank)
+            return min(stop + 1, ROPE_HEADS)
+
         parts = []
+        before_last, last = ROPE_UNITS - 2, ROPE_UNITS - 1
         for unit in range(ROPE_UNITS):
+            squared = square_through(unit, squared)
             parts.append(multiply_by_tables(unit))
             if unit == 0:
                 add(nc.gpsimd, unit, 0, 2)
                 add(nc.gpsimd, unit, 2, HEADS_PER_BANK)
-                store(unit)
-            elif unit < ROPE_UNITS - 2:
+            elif unit < before_last:
                 add(nc.gpsimd, unit, 0, HEADS_PER_BANK)
-                store(unit)
             if unit == 1:
-                filled = multiply_v()
-            if unit == V_AFTER:
-                copy_and_store_v(filled)
-        before_last, last = ROPE_UNITS - 2, ROPE_UNITS - 1
+                for g in range(V_BANKS - 1):
+                    multiply_v(g)
+                for g in range(Q_BANKS, ALL_BANKS):
+                    multiply_bank(g)
+                multiply_v(V_BANKS - 1)
+            if unit in V_STRETCHES:
+                start, stop = V_STRETCHES[unit]
+                copy_and_store_v(filled[start:stop])
+            if 0 < unit < last:
+                store(unit - 1, 0, HEADS_PER_BANK)
         add(nc.gpsimd, before_last, 0, 2)
         add(nc.vector, before_last, 2, HEADS_PER_BANK)
-        store(before_last)
-        add(nc.vector, last, 0, 2)
-        add(nc.vector, last, 2, HEADS_PER_BANK)
-        store(last)
+        store(before_last, 0, HEADS_PER_BANK)
+        for h in (0, 2):
+            add(nc.vector, last, h, h + 2)
+            store(last, h, h + 2)

@@ -63,8 +63,8 @@ def tile_multiheadattention_pa_s_kernel(
         identity = keep.tile([P, P], F32, name="identity")
         ones = keep.tile([P, P], BF16, name="ones")
         minus_ones = keep.tile([P, P], BF16, name="minus_ones")
-        gain_rows = keep.tile([P, 2, HEAD], BF16, name="gain_rows")
-        k_gains = keep.tile([P, 2, HEAD], F32, name="k_gains")
+        gain_rows = [keep.tile([P, HEAD], BF16, name="gain_row_%s" % label) for label in "qk"]
+        k_gain_sb = keep.tile([P, 3, HALF], F32, name="k_gain_sb")
         cos_sb = keep.tile([P, HEAD], BF16, name="cos_sb")
         sin_sb = keep.tile([P, HEAD], BF16, name="sin_sb")
         tables = keep.tile([P, 2, 2, HEAD], F32, name="tables")
@@ -85,11 +85,9 @@ def tile_multiheadattention_pa_s_kernel(
             plane_sb = keep.tile([P, cols], U8, name="plane_%s" % label, align_bytes=64)
             weights.append((words, scales, out, cols, words_sb, plane_sb))
 
-        nc.vector.memset(gain_rows[:], 0.0)
-        nc.vector.memset(weights[0][5][:].bitcast(I32), 0)
+        nc.vector.memset(gain_rows[0][:], 0.0)
+        nc.gpsimd.memset(gain_rows[1][:], 0.0)
         nc.vector.memset(eps[:], EPS)
-        nc.vector.memset(weights[1][5][:].bitcast(I32), 0)
-        nc.vector.memset(weights[2][5][:].bitcast(I32), 0)
         nc.vector.memset(ones[:], 1.0)
         nc.vector.memset(minus_ones[:], -1.0)
         make_identity(nc, identity[:])
@@ -110,8 +108,8 @@ def tile_multiheadattention_pa_s_kernel(
                     out=words_sb[:].bitcast(I32), in_=words.flatten_outer_dims().bitcast(I32)
                 )
 
-        nc.scalar.dma_start(out=gain_rows[0:1, 0, :], in_=q_scale.unsqueeze(0))
-        nc.scalar.dma_start(out=gain_rows[0:1, 1, :], in_=k_scale.unsqueeze(0))
+        nc.scalar.dma_start(out=gain_rows[0][0:1, :], in_=q_scale.unsqueeze(0))
+        nc.scalar.dma_start(out=gain_rows[1][0:1, :], in_=k_scale.unsqueeze(0))
         nc.sync.dma_start(out=x_sb[:], in_=hidden_states.flatten_outer_dims())
         load_weight(weights[0], True)
         nc.scalar.activation(out=table_warmer[:], in_=eps[:], func=ACT.Abs_reciprocal_sqrt)
@@ -124,34 +122,41 @@ def tile_multiheadattention_pa_s_kernel(
         x_pairs = psum.tile([P, 2, P], F32, name="x_pairs", tag="bank%d" % (ALL_BANKS - 1))
         for u in range(2):
             nc.tensor.transpose(x_pairs[:, u, :], x_words[:, u : K // 2 : 2], identity[:])
-        nc.vector.tensor_copy(
+        nc.scalar.copy(
             out=x_grouped[:].bitcast(F32).rearrange("p (s u) -> p s u", u=2),
             in_=x_pairs[:].rearrange("p u s -> p s u"),
         )
         nc.vector.quantize_mx(out=x_codes[:].bitcast(FP8X4), scales=x_plane[:], in_=x_grouped[:])
 
-        gains = psum.tile([P, 2, 2, HEAD], F32, name="gains", tag="bank%d" % (ALL_BANKS - 2))
-        for signs, out, row in (
-            (ones, gains[:, :, 0, :], gain_rows[:]),
-            (ones, gains[:, :, 1, 0:HALF], gain_rows[:, :, 0:HALF]),
-            (minus_ones, gains[:, :, 1, HALF:HEAD], gain_rows[:, :, HALF:HEAD]),
-        ):
-            nc.tensor.matmul(out=out, lhsT=signs[:], rhs=row, start=True, stop=True)
-        nc.scalar.copy(out=k_gains[:], in_=gains[:, 1])
-
-        def make_tables(engine, w, signed_gains):
-            engine.tensor_tensor(
-                out=tables[:, w, 0, :], in0=signed_gains[:, 0, :], in1=cos_sb[:], op=ALU.mult
+        def spread_gain(w):
+            gain = psum.tile([P, 3, HALF], F32, name="gain%d" % w, tag="bank%d" % (ALL_BANKS - 2 - w))
+            row = gain_rows[w]
+            nc.tensor.matmul(out=gain[:, 0:2, :], lhsT=ones[:], rhs=row[:], start=True, stop=True)
+            nc.tensor.matmul(
+                out=gain[:, 2, :], lhsT=minus_ones[:], rhs=row[:, HALF:HEAD], start=True, stop=True
             )
-            engine.tensor_tensor(
-                out=tables[:, w, 1, :].rearrange("p (t j) -> p t j", t=2),
-                in0=signed_gains[:, 1, :].rearrange("p (t j) -> p t j", t=2),
-                in1=sin_sb[:].rearrange("p (t j) -> p t j", t=2)[:, ::-1, :],
-                op=ALU.mult,
-            )
+            return gain
 
-        make_tables(nc.vector, 0, gains[:, 0])
-        make_tables(nc.gpsimd, 1, k_gains)
+        def make_tables(engine, w, gain):
+            for table, blocks, trig in (
+                (0, gain[:, 0:2, :], halves(cos_sb)),
+                (1, gain[:, 0:3:2, :], halves(sin_sb)[:, ::-1, :]),
+            ):
+                engine.tensor_tensor(
+                    out=tables[:, w, table, :].rearrange("p (t j) -> p t j", t=2),
+                    in0=blocks,
+                    in1=trig,
+                    op=ALU.mult,
+                )
+
+        def halves(trig):
+            return trig[:].rearrange("p (t j) -> p t j", t=2)
+
+        q_gain = spread_gain(0)
+        k_gain = spread_gain(1)
+        nc.scalar.copy(out=k_gain_sb[:], in_=k_gain[:])
+        make_tables(nc.vector, 0, q_gain)
+        make_tables(nc.gpsimd, 1, k_gain_sb)
 
         def multiply(which, c0, cols, product, p0):
             words, scales, out, all_cols, words_sb, plane_sb = weights[which]

@@ -24,10 +24,9 @@ ROPE_HEADS = (Q_COLS + K_COLS) // HEAD
 ROPE_UNITS = ROPE_HEADS // HEADS_PER_BANK
 ALL_BANKS = (Q_COLS + K_COLS + V_COLS) // BANK
 EPS = 1e-6
-V_STRETCHES = {2: (0, 1), 3: (1, 2), 4: (2, 4)}
+V_STRETCHES = {4: (0, 2), 5: (2, 4)}
 GROUP_HEADS = (1, 2, 2, 3, 4, 4, 4, 4)
 V_BANKS = 4
-Q_BANKS = 6
 
 FLOPS = 2 * P * K * (Q_COLS + K_COLS + V_COLS)
 
@@ -92,31 +91,34 @@ def tile_multiheadattention_pa_s_kernel(
         nc.vector.memset(minus_ones[:], -1.0)
         make_identity(nc, identity[:])
 
-        def load_weight(weight, words_first):
+        def load_words(weight, c0, c1):
             words, scales, out, cols, words_sb, plane_sb = weight
-            if words_first:
-                nc.sync.dma_start(
-                    out=words_sb[:].bitcast(I32), in_=words.flatten_outer_dims().bitcast(I32)
-                )
+            nc.sync.dma_start(
+                out=words_sb[:, 2 * c0 : 2 * c1].bitcast(I32),
+                in_=words.flatten_outer_dims()[:, 2 * c0 : 2 * c1].bitcast(I32),
+            )
+
+        def load_scales(weight):
+            words, scales, out, cols, words_sb, plane_sb = weight
             for r in range(4):
                 nc.sync.dma_start(
                     out=plane_sb[r:P:32, :].bitcast(I32),
                     in_=scales.flatten_outer_dims()[r:16:4, :].bitcast(I32),
                 )
-            if not words_first:
-                nc.sync.dma_start(
-                    out=words_sb[:].bitcast(I32), in_=words.flatten_outer_dims().bitcast(I32)
-                )
 
         nc.scalar.dma_start(out=gain_rows[0][0:1, :], in_=q_scale.unsqueeze(0))
         nc.scalar.dma_start(out=gain_rows[1][0:1, :], in_=k_scale.unsqueeze(0))
         nc.sync.dma_start(out=x_sb[:], in_=hidden_states.flatten_outer_dims())
-        load_weight(weights[0], True)
+        load_words(weights[0], 0, Q_COLS // 2)
+        load_scales(weights[0])
         nc.scalar.activation(out=table_warmer[:], in_=eps[:], func=ACT.Abs_reciprocal_sqrt)
         nc.sync.dma_start(out=cos_sb[:], in_=cos.flatten_outer_dims())
         nc.sync.dma_start(out=sin_sb[:], in_=sin.flatten_outer_dims())
-        load_weight(weights[2], False)
-        load_weight(weights[1], False)
+        load_words(weights[0], Q_COLS // 2, Q_COLS)
+        load_scales(weights[1])
+        load_words(weights[1], 0, K_COLS)
+        load_scales(weights[2])
+        load_words(weights[2], 0, V_COLS)
 
         x_words = x_sb[:].bitcast(F32)
         x_pairs = psum.tile([P, 2, P], F32, name="x_pairs", tag="bank%d" % (ALL_BANKS - 1))
@@ -189,7 +191,7 @@ def tile_multiheadattention_pa_s_kernel(
             which = 0 if first * HEAD < Q_COLS else 1
             multiply_heads(which, first - which * (Q_COLS // HEAD), GROUP_HEADS[g], product, 0)
 
-        for g in range(Q_BANKS):
+        for g in range(ALL_BANKS):
             multiply_bank(g)
 
         squares = keep.tile([P, ROPE_HEADS * HEAD], F32, name="squares")
@@ -287,16 +289,13 @@ def tile_multiheadattention_pa_s_kernel(
             elif unit < before_last:
                 add(nc.gpsimd, unit, 0, HEADS_PER_BANK)
             if unit == 1:
-                for g in range(V_BANKS - 1):
+                for g in range(V_BANKS):
                     multiply_v(g)
-                for g in range(Q_BANKS, ALL_BANKS):
-                    multiply_bank(g)
-                multiply_v(V_BANKS - 1)
             if unit in V_STRETCHES:
                 start, stop = V_STRETCHES[unit]
                 copy_and_store_v(filled[start:stop])
-            if 0 < unit < last:
-                store(unit - 1, 0, HEADS_PER_BANK)
+            if unit >= 2:
+                store(unit - 2, 0, HEADS_PER_BANK)
         add(nc.gpsimd, before_last, 0, 2)
         add(nc.vector, before_last, 2, HEADS_PER_BANK)
         store(before_last, 0, HEADS_PER_BANK)

from contextlib import ExitStack

import concourse.mybir as mybir
from concourse.masks import make_identity

F32 = mybir.dt.float32
BF16 = mybir.dt.bfloat16
I32 = mybir.dt.int32
U32 = mybir.dt.uint32
U8 = mybir.dt.uint8
FP8X4 = mybir.dt.float8_e4m3fn_x4
FP4X4 = mybir.dt.float4_e2m1fn_x4
ACT = mybir.ActivationFunctionType
ALU = mybir.AluOpType

P = 128
K = 512
HEAD = 128
HALF = HEAD // 2
BANK = 512
HEADS_PER_BANK = BANK // HEAD
Q_COLS, K_COLS, V_COLS = 2048, 1024, 1024
ROPE_HEADS = (Q_COLS + K_COLS) // HEAD
ROPE_UNITS = ROPE_HEADS // HEADS_PER_BANK
ALL_BANKS = (Q_COLS + K_COLS + V_COLS) // BANK
EPS = 1e-6
V_STRETCHES = {4: (0, 2), 5: (2, 4)}
GROUP_HEADS = (1, 2, 2, 3, 4, 4, 4, 4)
V_BANKS = 4

FLOPS = 2 * P * K * (Q_COLS + K_COLS + V_COLS)


def tile_multiheadattention_pa_s_kernel(
    tc,
    hidden_states,
    cos,
    sin,
    Wq_words,
    Wq_scales,
    Wk_words,
    Wk_scales,
    Wv_words,
    Wv_scales,
    q_scale,
    k_scale,
    out_0,
    out_1,
    out_2,
):
    nc = tc.nc
    with ExitStack() as ctx:
        keep = ctx.enter_context(tc.tile_pool(name="keep", bufs=1))
        work = ctx.enter_context(tc.tile_pool(name="work", bufs=ALL_BANKS))
        psum = ctx.enter_context(tc.psum_pool(name="psum", bufs=1))
        ctx.enter_context(tc.manual_schedule())

        x_sb = keep.tile([P, K], BF16, name="x_sb")
        x_grouped = keep.tile([P, K], BF16, name="x_grouped", align_bytes=64)
        x_codes = keep.tile([P, P], U32, name="x_codes", align_bytes=64)
        x_plane = keep.tile([P, P], U8, name="x_plane", align_bytes=64)
        identity = keep.tile([P, P], F32, name="identity")
        ones = keep.tile([P, P], BF16, name="ones")
        minus_ones = keep.tile([P, P], BF16, name="minus_ones")
        gain_rows = [keep.tile([P, HEAD], BF16, name="gain_row_%s" % label) for label in "qk"]
        k_gain_sb = keep.tile([P, 3, HALF], F32, name="k_gain_sb")
        cos_sb = keep.tile([P, HEAD], BF16, name="cos_sb")
        sin_sb = keep.tile([P, HEAD], BF16, name="sin_sb")
        tables = keep.tile([P, 2, 2, HEAD], F32, name="tables")
        eps = keep.tile([P, 1], F32, name="eps")
        table_warmer = keep.tile([P, 1], F32, name="table_warmer")
        sum_sq = keep.tile([P, ROPE_HEADS], F32, name="sum_sq")
        inv_rms = keep.tile([P, ROPE_HEADS], F32, name="inv_rms")
        values = keep.tile([P, V_COLS], F32, name="values")

        weights = []
        for label, words, scales, out in (
            ("q", Wq_words, Wq_scales, out_0),
            ("k", Wk_words, Wk_scales, out_1),
            ("v", Wv_words, Wv_scales, out_2),
        ):
            cols = scales.shape[2]
            words_sb = keep.tile([P, 2 * cols], U8, name="words_%s" % label, align_bytes=64)
            plane_sb = keep.tile([P, cols], U8, name="plane_%s" % label, align_bytes=64)
            weights.append((words, scales, out, cols, words_sb, plane_sb))

        nc.vector.memset(gain_rows[0][:], 0.0)
        nc.gpsimd.memset(gain_rows[1][:], 0.0)
        nc.vector.memset(eps[:], EPS)
        nc.vector.memset(ones[:], 1.0)
        nc.vector.memset(minus_ones[:], -1.0)
        make_identity(nc, identity[:])

        def load_words(weight, c0, c1):
            words, scales, out, cols, words_sb, plane_sb = weight
            nc.sync.dma_start(
                out=words_sb[:, 2 * c0 : 2 * c1].bitcast(I32),
                in_=words.flatten_outer_dims()[:, 2 * c0 : 2 * c1].bitcast(I32),
            )

        def load_scales(weight):
            words, scales, out, cols, words_sb, plane_sb = weight
            for r in range(4):
                nc.sync.dma_start(
                    out=plane_sb[r:P:32, :].bitcast(I32),
                    in_=scales.flatten_outer_dims()[r:16:4, :].bitcast(I32),
                )

        nc.scalar.dma_start(out=gain_rows[0][0:1, :], in_=q_scale.unsqueeze(0))
        nc.scalar.dma_start(out=gain_rows[1][0:1, :], in_=k_scale.unsqueeze(0))
        nc.sync.dma_start(out=x_sb[:], in_=hidden_states.flatten_outer_dims())
        load_words(weights[0], 0, Q_COLS // 2)
        load_scales(weights[0])
        nc.scalar.activation(out=table_warmer[:], in_=eps[:], func=ACT.Abs_reciprocal_sqrt)
        nc.sync.dma_start(out=cos_sb[:], in_=cos.flatten_outer_dims())
        nc.sync.dma_start(out=sin_sb[:], in_=sin.flatten_outer_dims())
        load_words(weights[0], Q_COLS // 2, Q_COLS)
        load_scales(weights[1])
        load_words(weights[1], 0, K_COLS)
        load_scales(weights[2])
        load_words(weights[2], 0, V_COLS)

        x_words = x_sb[:].bitcast(F32)
        x_pairs = psum.tile([P, 2, P], F32, name="x_pairs", tag="bank%d" % (ALL_BANKS - 1))
        for u in range(2):
            nc.tensor.transpose(x_pairs[:, u, :], x_words[:, u : K // 2 : 2], identity[:])
        nc.scalar.copy(
            out=x_grouped[:].bitcast(F32).rearrange("p (s u) -> p s u", u=2),
            in_=x_pairs[:].rearrange("p u s -> p s u"),
        )
        nc.vector.quantize_mx(out=x_codes[:].bitcast(FP8X4), scales=x_plane[:], in_=x_grouped[:])

        def spread_gain(w):
            gain = psum.tile([P, 3, HALF], F32, name="gain%d" % w, tag="bank%d" % (ALL_BANKS - 2 - w))
            row = gain_rows[w]
            nc.tensor.matmul(out=gain[:, 0:2, :], lhsT=ones[:], rhs=row[:], start=True, stop=True)
            nc.tensor.matmul(
                out=gain[:, 2, :], lhsT=minus_ones[:], rhs=row[:, HALF:HEAD], start=True, stop=True
            )
            return gain

        def make_tables(engine, w, gain):
            for table, blocks, trig in (
                (0, gain[:, 0:2, :], halves(cos_sb)),
                (1, gain[:, 0:3:2, :], halves(sin_sb)[:, ::-1, :]),
            ):
                engine.tensor_tensor(
                    out=tables[:, w, table, :].rearrange("p (t j) -> p t j", t=2),
                    in0=blocks,
                    in1=trig,
                    op=ALU.mult,
                )

        def halves(trig):
            return trig[:].rearrange("p (t j) -> p t j", t=2)

        q_gain = spread_gain(0)
        k_gain = spread_gain(1)
        nc.scalar.copy(out=k_gain_sb[:], in_=k_gain[:])
        make_tables(nc.vector, 0, q_gain)
        make_tables(nc.gpsimd, 1, k_gain_sb)

        def multiply(which, c0, cols, product, p0):
            words, scales, out, all_cols, words_sb, plane_sb = weights[which]
            nc.tensor.matmul_mx(
                out=product[:, p0 : p0 + cols],
                lhsT=x_codes[:].bitcast(FP8X4),
                lhsT_scale=x_plane[:],
                rhs=words_sb[:, 2 * c0 : 2 * (c0 + cols)].bitcast(FP4X4),
                rhs_scale=plane_sb[:, c0 : c0 + cols],
                start=True,
                stop=True,
            )

        def multiply_heads(which, first, heads, product, p0):
            while heads > 0:
                n = 4 if heads == 4 else min(heads, 2)
                multiply(which, first * HEAD, n * HEAD, product, p0)
                first, heads, p0 = first + n, heads - n, p0 + n * HEAD

        banks = []
        place = []
        for g, heads in enumerate(GROUP_HEADS):
            for h in range(heads):
                place.append((g, h * HEAD))

        def multiply_bank(g):
            first = sum(GROUP_HEADS[:g])
            product = psum.tile([P, BANK], F32, name="product%d" % g, tag="bank%d" % g)
            banks.append(product)
            which = 0 if first * HEAD < Q_COLS else 1
            multiply_heads(which, first - which * (Q_COLS // HEAD), GROUP_HEADS[g], product, 0)

        for g in range(ALL_BANKS):
            multiply_bank(g)

        squares = keep.tile([P, ROPE_HEADS * HEAD], F32, name="squares")

        def sum_squares(head):
            g, p0 = place[head]
            nc.scalar.activation(
                out=squares[:, head * HEAD : (head + 1) * HEAD],
                in_=banks[g][:, p0 : p0 + HEAD],
                func=ACT.Square,
                accum_out=sum_sq[:, head : head + 1],
            )

        def inverse_rms(g):
            heads = [h for h in range(ROPE_HEADS) if place[h][0] == g]
            nc.scalar.activation(
                out=inv_rms[:, heads[0] : heads[-1] + 1],
                in_=sum_sq[:, heads[0] : heads[-1] + 1],
                func=ACT.Abs_reciprocal_sqrt,
                scale=1.0 / HEAD,
                bias=eps[:],
            )

        def multiply_by_tables(unit):
            which = 0 if unit * BANK < Q_COLS else 1
            c0 = unit * BANK - which * Q_COLS
            out_cols = weights[which][2].rearrange("b s h d -> (b s) (h d)")[:, c0 : c0 + BANK]
            stay_cross = work.tile([P, HEADS_PER_BANK, 2, 2, HALF], F32, name="stay_cross")
            rotated = work.tile([P, HEADS_PER_BANK, 2, HALF], F32, name="rotated")
            for h in range(HEADS_PER_BANK):
                head = unit * HEADS_PER_BANK + h
                g, p0 = place[head]
                nc.vector.scalar_tensor_tensor(
                    out=stay_cross[:, h].rearrange("p w t j -> p w (t j)"),
                    in0=banks[g][:, p0 : p0 + HEAD].unsqueeze(1).to_broadcast([P, 2, HEAD]),
                    scalar=inv_rms[:, head : head + 1],
                    in1=tables[:, which],
                    op0=ALU.mult,
                    op1=ALU.mult,
                )
            return stay_cross, rotated, out_cols

        def add(engine, unit, h0, h1):
            stay_cross, rotated, out_cols = parts[unit]
            engine.tensor_tensor(
                out=rotated[:, h0:h1],
                in0=stay_cross[:, h0:h1, 0, :, :],
                in1=stay_cross[:, h0:h1, 1, ::-1, :],
                op=ALU.add,
            )

        def store(unit, h0, h1):
            stay_cross, rotated, out_cols = parts[unit]
            nc.sync.dma_start(
                out=out_cols[:, h0 * HEAD : h1 * HEAD],
                in_=rotated[:, h0:h1].rearrange("p h t j -> p (h t j)"),
            )

        filled = []

        def multiply_v(g):
            free = HEADS_PER_BANK - GROUP_HEADS[g]
            first = sum(HEADS_PER_BANK - heads for heads in GROUP_HEADS[:g])
            filled.append((g, GROUP_HEADS[g] * HEAD, free * HEAD, first * HEAD))
            multiply_heads(2, first, free, banks[g], GROUP_HEADS[g] * HEAD)

        def copy_and_store_v(stretches):
            out_rows = weights[2][2].rearrange("b s h d -> (b s) (h d)")
            for g, p0, cols, c0 in stretches:
                nc.scalar.copy(out=values[:, c0 : c0 + cols], in_=banks[g][:, p0 : p0 + cols])
            start, stop = stretches[0][3], stretches[-1][3] + stretches[-1][2]
            nc.sync.dma_start(out=out_rows[:, start:stop], in_=values[:, start:stop])

        squared = 0

        def square_through(unit, squared):
            last_bank = place[unit * HEADS_PER_BANK + HEADS_PER_BANK - 1][0]
            stop = sum(GROUP_HEADS[: last_bank + 1])
            for head in range(squared, min(stop + 1, ROPE_HEADS)):
                sum_squares(head)
                if head > 0 and place[head][0] != place[head - 1][0]:
                    inverse_rms(place[head - 1][0])
            if stop == ROPE_HEADS:
                inverse_rms(last_bank)
            return min(stop + 1, ROPE_HEADS)

        parts = []
        before_last, last = ROPE_UNITS - 2, ROPE_UNITS - 1
        for unit in range(ROPE_UNITS):
            squared = square_through(unit, squared)
            parts.append(multiply_by_tables(unit))
            if unit == 0:
                add(nc.gpsimd, unit, 0, 2)
                add(nc.gpsimd, unit, 2, HEADS_PER_BANK)
            elif unit < before_last:
                add(nc.gpsimd, unit, 0, HEADS_PER_BANK)
            if unit == 1:
                for g in range(V_BANKS):
                    multiply_v(g)
            if unit in V_STRETCHES:
                start, stop = V_STRETCHES[unit]
                copy_and_store_v(filled[start:stop])
            if unit >= 2:
                store(unit - 2, 0, HEADS_PER_BANK)
        add(nc.gpsimd, before_last, 0, 2)
        add(nc.vector, before_last, 2, HEADS_PER_BANK)
        store(before_last, 0, HEADS_PER_BANK)
        for h in (0, 2):
            add(nc.vector, last, h, h + 2)
            store(last, h, h + 2)
